import numpy as np
import ml_dtypes


BF16 = ml_dtypes.bfloat16


def bf(x):
    return np.asarray(x, np.float32).astype(BF16)


def f64(x):
    return np.asarray(x).astype(np.float64)


E2M1 = np.array([0.0, 0.5, 1.0, 1.5, 2.0, 3.0, 4.0, 6.0, -0.0, -0.5, -1.0, -1.5, -2.0, -3.0, -4.0, -6.0])


def pack_weight(w, fmt):
    k, n = w.shape
    w = f64(bf(w)).reshape(k // 32, 32, n)
    amax = np.abs(w).max(1)
    if fmt == "e4m3":
        byte = np.frexp(amax)[1] - 1 + 127 - 7
    else:
        mant, ex = np.frexp(amax / 6.0)
        byte = np.where(mant > 0.5, ex, ex - 1) + 127
    byte = np.clip(np.where(amax > 0, byte, 1), 1, 254)
    scaled = (w * np.exp2(127.0 - byte)[:, None, :]).reshape(k, n).astype(np.float32)
    by_word = np.ascontiguousarray(scaled.reshape(k // 512, 128, 4, n).transpose(0, 1, 3, 2))
    if fmt == "e4m3":
        words = by_word.astype(ml_dtypes.float8_e4m3fn).view(np.uint8)
    else:
        c = by_word.astype(ml_dtypes.float4_e2m1fn).view(np.uint8) & 0xF
        words = c[..., 0::2] | (c[..., 1::2] << 4)
    return np.ascontiguousarray(words), np.ascontiguousarray(byte.astype(np.uint8).reshape(k // 512, 16, n))


def unpack_weight(words, scales, fmt):
    g, p, n, _ = words.shape
    if fmt == "e4m3":
        vals = np.ascontiguousarray(words).view(ml_dtypes.float8_e4m3fn).astype(np.float64)
    else:
        nib = np.empty((g, p, n, 4), np.uint8)
        nib[..., 0::2] = words & 0xF
        nib[..., 1::2] = words >> 4
        vals = E2M1[nib]
    vals = vals * np.repeat(np.exp2(scales.astype(np.float64) - 127.0), 8, axis=1)[..., None]
    return vals.transpose(0, 1, 3, 2).reshape(g * 512, n)

def pack4(w):
    words, scales = pack_weight(w, "e2m1")
    return words.reshape(words.shape[0], 128, -1), scales


def unpack4(words, scales):
    return unpack_weight(words.reshape(words.shape[0], 128, -1, 2), scales, "e2m1")


def kspread(k):
    return np.exp2(np.repeat(np.random.randint(-6, 7, k // 32), 32).astype(np.float64))


B, T, C, H = 4, 128, 4096, 32
HD = C // H


def rotary_pos_emb(v):
    exponents = f64(np.arange(0, HD, 2)[: HD // 2] // HD)
    freqs = 1.0 / np.power(1000.0, exponents)
    theta = f64(np.arange(T))[:, None] * freqs[None, :]
    cos = np.cos(theta)[None, :, None, :]
    sin = np.sin(theta)[None, :, None, :]
    vr = v.reshape(B, T, H, HD // 2, 2)
    v0, v1 = vr[..., 0], vr[..., 1]
    out = np.stack([v0 * cos - v1 * sin, v0 * sin + v1 * cos], axis=-1)
    return out.reshape(B, T, H, HD)


def setup_inputs():
    s = kspread(C)
    x = np.random.standard_normal((B, T, C)) * s
    wq = np.random.standard_normal((C, C)) / np.sqrt(C) / s[None, :]
    wk = np.random.standard_normal((C, C)) / np.sqrt(C) / s[None, :]
    x_words, x_scales = pack4(np.ascontiguousarray(x.reshape(B * T, C).T))
    wq_words, wq_scales = pack4(np.ascontiguousarray(wq.T))
    wk_words, wk_scales = pack4(np.ascontiguousarray(wk.T))
    return {"x_words": x_words, "x_scales": x_scales,
            "wq_words": wq_words, "wq_scales": wq_scales,
            "wk_words": wk_words, "wk_scales": wk_scales}


def reference(x_words, x_scales, wq_words, wq_scales, wk_words, wk_scales):
    xm = unpack4(x_words, x_scales).T.reshape(B, T, C)
    q = (xm @ unpack4(wq_words, wq_scales)).reshape(B, T, H, HD)
    k = (xm @ unpack4(wk_words, wk_scales)).reshape(B, T, H, HD)
    return rotary_pos_emb(q), rotary_pos_emb(k)

@@ -1,0 +1,190 @@
+import math
+from contextlib import ExitStack
+
+import concourse.mybir as mybir
+
+F32 = mybir.dt.float32
+BF16 = mybir.dt.bfloat16
+I32 = mybir.dt.int32
+U8 = mybir.dt.uint8
+FP4X4 = mybir.dt.float4_e2m1fn_x4
+ALU = mybir.AluOpType
+ACT = mybir.ActivationFunctionType
+
+P = 128
+PASSES = 8
+TOKEN_TILES = 4
+BANK = 512
+CHUNK = 1024
+CHUNKS = 8
+AHEAD = 2
+WARM = 7
+TAIL = (256, 128, 128,)
+
+FLOPS = 2 * 512 * 4096 * 8192
+
+TWO_PI_HIGH = 6.28125
+TWO_PI_LOW = 2.0 * math.pi - TWO_PI_HIGH
+
+
+def tile_attention_pa_kernel(tc, x_words, x_scales, wq_words, wq_scales, wk_words, wk_scales, out_0, out_1):
+    nc = tc.nc
+    with ExitStack() as ctx:
+        keep = ctx.enter_context(tc.tile_pool(name="keep", bufs=1))
+        swap_pool = ctx.enter_context(tc.tile_pool(name="swap", bufs=3))
+        res_pool = ctx.enter_context(tc.tile_pool(name="res", bufs=6))
+        psum = ctx.enter_context(tc.psum_pool(name="psum", bufs=8))
+        ctx.enter_context(tc.manual_schedule())
+
+        def alloc_runs(label, runs, width):
+            where = {}
+            for g0, g1 in runs:
+                t = keep.tile([P, g1 - g0, width], U8, name="%s_%d" % (label, g0), align_bytes=64)
+                for g in range(g0, g1):
+                    where[g] = (t, g - g0)
+            return where
+
+        def load_codes(words, where, g0, g1, b0, width):
+            nc.sync.dma_start(
+                out=where[g0][0][:].bitcast(I32),
+                in_=words[g0:g1, :, b0 : b0 + width].rearrange("g p b -> p g b").bitcast(I32),
+            )
+
+        def load_planes(scales, where, g0, g1, c0, width):
+            t = where[g0][0]
+            nc.vector.memset(t[:].rearrange("p g c -> p (g c)").bitcast(I32), 0)
+            for q in range(4):
+                nc.sync.dma_start(
+                    out=t[32 * q : 32 * q + 4, :, :].bitcast(I32),
+                    in_=scales[g0:g1, 4 * q : 4 * q + 4, c0 : c0 + width].rearrange("g r c -> r g c").bitcast(I32),
+                )
+
+        def chunk_source(c):
+            if c < CHUNKS // 2:
+                return wq_words, wq_scales, out_0, CHUNK * c
+            return wk_words, wk_scales, out_1, CHUNK * (c - CHUNKS // 2)
+
+        pos = keep.tile([P, 1], F32, name="pos")
+        nc.gpsimd.iota(pos[:], pattern=[[0, 1]], base=0, channel_multiplier=1, allow_small_or_imprecise_dtypes=True)
+        odd = keep.tile([P, 20], F32, name="odd")
+        nc.gpsimd.iota(odd[:], pattern=[[2, 20]], base=1, channel_multiplier=0, allow_small_or_imprecise_dtypes=True)
+
+        x_codes = alloc_runs("xc", ((0, 1), (1, 4), (4, 8)), 2 * 512)
+        x_planes = alloc_runs("xp", ((0, 4), (4, 8)), 512)
+        w_codes = {0: alloc_runs("wc0", ((0, 1), (1, 2), (2, 4), (4, 8)), 2 * CHUNK)}
+        w_planes = {0: alloc_runs("wp0", ((0, 1), (1, 4), (4, 8)), CHUNK)}
+        for c in range(1, CHUNKS):
+            w_codes[c] = alloc_runs("wc%d" % c, ((0, 4), (4, 8)), 2 * CHUNK)
+            w_planes[c] = alloc_runs("wp%d" % c, ((0, 8),), CHUNK)
+
+        def load_chunk(c):
+            words, scales, unused_out, c0 = chunk_source(c)
+            load_planes(scales, w_planes[c], 0, 8, c0, CHUNK)
+            load_codes(words, w_codes[c], 0, 4, 2 * c0, 2 * CHUNK)
+            load_codes(words, w_codes[c], 4, 8, 2 * c0, 2 * CHUNK)
+
+        zeros = keep.tile([P, BANK], BF16, name="zeros")
+        nc.vector.memset(zeros[:], 0.0)
+        load_codes(wq_words, w_codes[0], 0, 1, 0, 2 * CHUNK)
+        load_codes(x_words, x_codes, 0, 1, 0, 2 * 512)
+        load_planes(wq_scales, w_planes[0], 0, 1, 0, CHUNK)
+        load_planes(x_scales, x_planes, 0, 4, 0, 512)
+
+        if WARM > 0:
+            idle = psum.tile([P, BANK], F32, name="acc", tag="acc")
+            for i in range(WARM):
+                nc.tensor.matmul(out=idle[:], lhsT=zeros[:, 0:P], rhs=zeros[:], start=True, stop=True)
+
+        load_codes(wq_words, w_codes[0], 1, 2, 0, 2 * CHUNK)
+        load_codes(x_words, x_codes, 1, 4, 0, 2 * 512)
+        load_planes(wq_scales, w_planes[0], 1, 4, 0, CHUNK)
+        load_codes(wq_words, w_codes[0], 2, 4, 0, 2 * CHUNK)
+        load_codes(wq_words, w_codes[0], 4, 8, 0, 2 * CHUNK)
+        load_codes(x_words, x_codes, 4, 8, 0, 2 * 512)
+        load_planes(wq_scales, w_planes[0], 4, 8, 0, CHUNK)
+        load_planes(x_scales, x_planes, 4, 8, 0, 512)
+
+        passed = keep.tile([P, 20], F32, name="passed")
+        nc.vector.tensor_scalar(out=passed[:], in0=odd[:], scalar1=math.pi, scalar2=pos[:, 0:1], op0=ALU.mult, op1=ALU.is_le)
+        turns = keep.tile([P, 1], F32, name="turns")
+        nc.vector.tensor_reduce(out=turns[:], in_=passed[:], axis=mybir.AxisListType.X, op=ALU.add)
+        coarse = keep.tile([P, 1], F32, name="coarse")
+        nc.vector.scalar_tensor_tensor(out=coarse[:], in0=turns[:], scalar=-TWO_PI_HIGH, in1=pos[:], op0=ALU.mult, op1=ALU.add)
+        angles = keep.tile([P, 2], F32, name="angles")
+        nc.vector.scalar_tensor_tensor(out=angles[:, 0:1], in0=turns[:], scalar=-TWO_PI_LOW, in1=coarse[:], op0=ALU.mult, op1=ALU.add)
+        size = keep.tile([P, 1], F32, name="size")
+        nc.vector.scalar_tensor_tensor(out=size[:], in0=angles[:, 0:1], scalar=-1.0, in1=angles[:, 0:1], op0=ALU.mult, op1=ALU.max)
+        nc.vector.tensor_scalar(out=angles[:, 1:2], in0=size[:], scalar1=-1.0, scalar2=math.pi / 2.0, op0=ALU.mult, op1=ALU.add)
+        trig = keep.tile([P, 2], F32, name="trig")
+        nc.scalar.activation(out=trig[:], in_=angles[:], func=ACT.Sin)
+        minus_sin = keep.tile([P, 1], F32, name="minus_sin")
+        nc.vector.tensor_scalar(out=minus_sin[:], in0=trig[:, 0:1], scalar1=-1.0, scalar2=None, op0=ALU.mult)
+        sin = trig[:, 0:1]
+        cos = trig[:, 1:2]
+
+        for c in range(1, 1 + AHEAD):
+            load_chunk(c)
+
+        def mx_pass(acc, width, m, g, c, col):
+            xc, xi = x_codes[g]
+            xp, xj = x_planes[g]
+            wc, wi = w_codes[c][g]
+            wp, wj = w_planes[c][g]
+            nc.tensor.matmul_mx(
+                out=acc[:, 0:width],
+                lhsT=xc[:, xi, 2 * P * m : 2 * P * (m + 1)].bitcast(FP4X4),
+                lhsT_scale=xp[:, xj, P * m : P * (m + 1)],
+                rhs=wc[:, wi, 2 * col : 2 * (col + width)].bitcast(FP4X4),
+                rhs_scale=wp[:, wj, col : col + width],
+                start=(g == 0),
+                stop=(g == PASSES - 1),
+            )
+
+        def rotate_and_store(acc, width, m, c, col):
+            unused_words, unused_scales, out, c0 = chunk_source(c)
+            half = width // 2
+            pairs = acc[:, 0:width].rearrange("p (i t) -> p i t", t=2)
+            swapped = swap_pool.tile([P, 2, half], F32, name="swapped", tag="swapped")
+            nc.scalar.activation(out=swapped[:, 0, :], in_=pairs[:, :, 1], func=ACT.Copy, scale=minus_sin[:, 0:1])
+            nc.scalar.activation(out=swapped[:, 1, :], in_=pairs[:, :, 0], func=ACT.Copy, scale=sin)
+            res = res_pool.tile([P, width], F32, name="res", tag="res")
+            nc.vector.scalar_tensor_tensor(
+                out=res[:].rearrange("p (i t) -> p i t", t=2),
+                in0=pairs,
+                scalar=cos,
+                in1=swapped[:].rearrange("p t i -> p i t"),
+                op0=ALU.mult,
+                op1=ALU.add,
+            )
+            nc.sync.dma_start(
+                out=out[m].rearrange("t h d -> t (h d)")[:, c0 + col : c0 + col + width],
+                in_=res[:],
+            )
+
+        first = []
+        for j in range(CHUNK // BANK):
+            for m in range(TOKEN_TILES):
+                acc = psum.tile([P, BANK], F32, name="acc", tag="acc")
+                first.append((acc, m, BANK * j))
+        for g in range(PASSES):
+            for acc, m, col in first:
+                mx_pass(acc, BANK, m, g, 0, col)
+        for acc, m, col in first:
+            rotate_and_store(acc, BANK, m, 0, col)
+        if 1 + AHEAD < CHUNKS:
+            load_chunk(1 + AHEAD)
+
+        for c in range(1, CHUNKS):
+            for j in range(CHUNK // BANK):
+                for m in range(TOKEN_TILES):
+                    last = c == CHUNKS - 1 and j == CHUNK // BANK - 1 and m == TOKEN_TILES - 1
+                    widths = TAIL if last else (BANK,)
+                    col = BANK * j
+                    for width in widths:
+                        acc = psum.tile([P, BANK], F32, name="acc", tag="acc")
+                        for g in range(PASSES):
+                            mx_pass(acc, width, m, g, c, col)
+                        rotate_and_store(acc, width, m, c, col)
+                        col += width
+            if c + 1 + AHEAD < CHUNKS:
+                load_chunk(c + 1 + AHEAD)

@@ -39,7 +39,7 @@ def tile_attention_pa_kernel(tc, x_words, x_scales, wq_words, wq_scales, wk_word
         def alloc_runs(label, runs, width):
             where = {}
             for g0, g1 in runs:
-                t = keep.tile([P, g1 - g0, width], U8, name="%s_%d" % (label, g0), align_bytes=64)
+                t = keep.tile([P, g1 - g0, width], U8, name="%s_%d" % (label, g0), align_bytes=256)
                 for g in range(g0, g1):
                     where[g] = (t, g - g0)
             return where

@@ -15,10 +15,9 @@ P = 128
 PASSES = 8
 TOKEN_TILES = 4
 BANK = 512
-CHUNK = 1024
-CHUNKS = 8
-AHEAD = 2
-WARM = 7
+UNITS = 16
+LEAD = 4
+WARM = 9
 TAIL = (256, 128, 128,)
 
 FLOPS = 2 * 512 * 4096 * 8192
@@ -31,15 +30,16 @@ def tile_attention_pa_kernel(tc, x_words, x_scales, wq_words, wq_scales, wk_word
     nc = tc.nc
     with ExitStack() as ctx:
         keep = ctx.enter_context(tc.tile_pool(name="keep", bufs=1))
+        raw_pool = ctx.enter_context(tc.tile_pool(name="raw", bufs=3))
         swap_pool = ctx.enter_context(tc.tile_pool(name="swap", bufs=3))
-        res_pool = ctx.enter_context(tc.tile_pool(name="res", bufs=6))
+        res_pool = ctx.enter_context(tc.tile_pool(name="res", bufs=5))
         psum = ctx.enter_context(tc.psum_pool(name="psum", bufs=8))
         ctx.enter_context(tc.manual_schedule())
 
         def alloc_runs(label, runs, width):
             where = {}
             for g0, g1 in runs:
-                t = keep.tile([P, g1 - g0, width], U8, name="%s_%d" % (label, g0), align_bytes=256)
+                t = keep.tile([P, g1 - g0, width], U8, name="%s_%d" % (label, g0), align_bytes=64)
                 for g in range(g0, g1):
                     where[g] = (t, g - g0)
             return where
@@ -59,10 +59,10 @@ def tile_attention_pa_kernel(tc, x_words, x_scales, wq_words, wq_scales, wk_word
                     in_=scales[g0:g1, 4 * q : 4 * q + 4, c0 : c0 + width].rearrange("g r c -> r g c").bitcast(I32),
                 )
 
-        def chunk_source(c):
-            if c < CHUNKS // 2:
-                return wq_words, wq_scales, out_0, CHUNK * c
-            return wk_words, wk_scales, out_1, CHUNK * (c - CHUNKS // 2)
+        def unit_source(n):
+            if n < UNITS // 2:
+                return wq_words, wq_scales, out_0, BANK * n
+            return wk_words, wk_scales, out_1, BANK * (n - UNITS // 2)
 
         pos = keep.tile([P, 1], F32, name="pos")
         nc.gpsimd.iota(pos[:], pattern=[[0, 1]], base=0, channel_multiplier=1, allow_small_or_imprecise_dtypes=True)
@@ -70,39 +70,38 @@ def tile_attention_pa_kernel(tc, x_words, x_scales, wq_words, wq_scales, wk_word
         nc.gpsimd.iota(odd[:], pattern=[[2, 20]], base=1, channel_multiplier=0, allow_small_or_imprecise_dtypes=True)
 
         x_codes = alloc_runs("xc", ((0, 1), (1, 4), (4, 8)), 2 * 512)
-        x_planes = alloc_runs("xp", ((0, 4), (4, 8)), 512)
-        w_codes = {0: alloc_runs("wc0", ((0, 1), (1, 2), (2, 4), (4, 8)), 2 * CHUNK)}
-        w_planes = {0: alloc_runs("wp0", ((0, 1), (1, 4), (4, 8)), CHUNK)}
-        for c in range(1, CHUNKS):
-            w_codes[c] = alloc_runs("wc%d" % c, ((0, 4), (4, 8)), 2 * CHUNK)
-            w_planes[c] = alloc_runs("wp%d" % c, ((0, 8),), CHUNK)
+        x_planes = alloc_runs("xp", ((0, 8),), 512)
+        pair_codes = alloc_runs("wc01", ((0, 1), (1, 2), (2, 4), (4, 6), (6, 8)), 4 * BANK)
+        pair_planes = alloc_runs("wp01", ((0, 2), (2, 8)), 2 * BANK)
+        w_codes = {}
+        w_planes = {}
+        for n in range(2, UNITS):
+            w_codes[n] = alloc_runs("wc%d" % n, ((0, 8),), 2 * BANK)
+            w_planes[n] = alloc_runs("wp%d" % n, ((0, 8),), BANK)
 
-        def load_chunk(c):
-            words, scales, unused_out, c0 = chunk_source(c)
-            load_planes(scales, w_planes[c], 0, 8, c0, CHUNK)
-            load_codes(words, w_codes[c], 0, 4, 2 * c0, 2 * CHUNK)
-            load_codes(words, w_codes[c], 4, 8, 2 * c0, 2 * CHUNK)
+        def load_unit(n):
+            words, scales, unused_out, c0 = unit_source(n)
+            load_planes(scales, w_planes[n], 0, 8, c0, BANK)
+            load_codes(words, w_codes[n], 0, 8, 2 * c0, 2 * BANK)
 
         zeros = keep.tile([P, BANK], BF16, name="zeros")
         nc.vector.memset(zeros[:], 0.0)
-        load_codes(wq_words, w_codes[0], 0, 1, 0, 2 * CHUNK)
+        load_codes(wq_words, pair_codes, 0, 1, 0, 4 * BANK)
         load_codes(x_words, x_codes, 0, 1, 0, 2 * 512)
-        load_planes(wq_scales, w_planes[0], 0, 1, 0, CHUNK)
-        load_planes(x_scales, x_planes, 0, 4, 0, 512)
+        load_planes(wq_scales, pair_planes, 0, 2, 0, 2 * BANK)
+        load_planes(x_scales, x_planes, 0, 8, 0, 512)
 
-        if WARM > 0:
-            idle = psum.tile([P, BANK], F32, name="acc", tag="acc")
-            for i in range(WARM):
-                nc.tensor.matmul(out=idle[:], lhsT=zeros[:, 0:P], rhs=zeros[:], start=True, stop=True)
+        idle = psum.tile([P, BANK], F32, name="acc", tag="acc")
+        for i in range(WARM):
+            nc.tensor.matmul(out=idle[:], lhsT=zeros[:, 0:P], rhs=zeros[:], start=True, stop=True)
 
-        load_codes(wq_words, w_codes[0], 1, 2, 0, 2 * CHUNK)
+        load_codes(wq_words, pair_codes, 1, 2, 0, 4 * BANK)
         load_codes(x_words, x_codes, 1, 4, 0, 2 * 512)
-        load_planes(wq_scales, w_planes[0], 1, 4, 0, CHUNK)
-        load_codes(wq_words, w_codes[0], 2, 4, 0, 2 * CHUNK)
-        load_codes(wq_words, w_codes[0], 4, 8, 0, 2 * CHUNK)
+        load_planes(wq_scales, pair_planes, 2, 8, 0, 2 * BANK)
+        load_codes(wq_words, pair_codes, 2, 4, 0, 4 * BANK)
+        load_codes(wq_words, pair_codes, 4, 6, 0, 4 * BANK)
         load_codes(x_words, x_codes, 4, 8, 0, 2 * 512)
-        load_planes(wq_scales, w_planes[0], 4, 8, 0, CHUNK)
-        load_planes(x_scales, x_planes, 4, 8, 0, 512)
+        load_codes(wq_words, pair_codes, 6, 8, 0, 4 * BANK)
 
         passed = keep.tile([P, 20], F32, name="passed")
         nc.vector.tensor_scalar(out=passed[:], in0=odd[:], scalar1=math.pi, scalar2=pos[:, 0:1], op0=ALU.mult, op1=ALU.is_le)
@@ -122,14 +121,19 @@ def tile_attention_pa_kernel(tc, x_words, x_scales, wq_words, wq_scales, wk_word
         sin = trig[:, 0:1]
         cos = trig[:, 1:2]
 
-        for c in range(1, 1 + AHEAD):
-            load_chunk(c)
+        for n in range(2, 2 + LEAD):
+            load_unit(n)
 
-        def mx_pass(acc, width, m, g, c, col):
+        def mx_pass(acc, width, m, g, n, col):
             xc, xi = x_codes[g]
             xp, xj = x_planes[g]
-            wc, wi = w_codes[c][g]
-            wp, wj = w_planes[c][g]
+            if n < 2:
+                wc, wi = pair_codes[g]
+                wp, wj = pair_planes[g]
+                col = col + BANK * n
+            else:
+                wc, wi = w_codes[n][g]
+                wp, wj = w_planes[n][g]
             nc.tensor.matmul_mx(
                 out=acc[:, 0:width],
                 lhsT=xc[:, xi, 2 * P * m : 2 * P * (m + 1)].bitcast(FP4X4),
@@ -140,10 +144,15 @@ def tile_attention_pa_kernel(tc, x_words, x_scales, wq_words, wq_scales, wk_word
                 stop=(g == PASSES - 1),
             )
 
-        def rotate_and_store(acc, width, m, c, col):
-            unused_words, unused_scales, out, c0 = chunk_source(c)
+        def rotate_and_store(acc, width, m, n, col):
+            unused_words, unused_scales, out, c0 = unit_source(n)
             half = width // 2
-            pairs = acc[:, 0:width].rearrange("p (i t) -> p i t", t=2)
+            if width == BANK:
+                raw = raw_pool.tile([P, width], F32, name="raw", tag="raw")
+                nc.scalar.copy(out=raw[:], in_=acc[:, 0:width])
+                pairs = raw[:].rearrange("p (i t) -> p i t", t=2)
+            else:
+                pairs = acc[:, 0:width].rearrange("p (i t) -> p i t", t=2)
             swapped = swap_pool.tile([P, 2, half], F32, name="swapped", tag="swapped")
             nc.scalar.activation(out=swapped[:, 0, :], in_=pairs[:, :, 1], func=ACT.Copy, scale=minus_sin[:, 0:1])
             nc.scalar.activation(out=swapped[:, 1, :], in_=pairs[:, :, 0], func=ACT.Copy, scale=sin)
@@ -162,29 +171,28 @@ def tile_attention_pa_kernel(tc, x_words, x_scales, wq_words, wq_scales, wk_word
             )
 
         first = []
-        for j in range(CHUNK // BANK):
+        for n in range(2):
             for m in range(TOKEN_TILES):
                 acc = psum.tile([P, BANK], F32, name="acc", tag="acc")
-                first.append((acc, m, BANK * j))
+                first.append((acc, m, n))
         for g in range(PASSES):
-            for acc, m, col in first:
-                mx_pass(acc, BANK, m, g, 0, col)
-        for acc, m, col in first:
-            rotate_and_store(acc, BANK, m, 0, col)
-        if 1 + AHEAD < CHUNKS:
-            load_chunk(1 + AHEAD)
+            for acc, m, n in first:
+                mx_pass(acc, BANK, m, g, n, 0)
+        for acc, m, n in first:
+            rotate_and_store(acc, BANK, m, n, 0)
+        for n in range(2 + LEAD, min(4 + LEAD, UNITS)):
+            load_unit(n)
 
-        for c in range(1, CHUNKS):
-            for j in range(CHUNK // BANK):
-                for m in range(TOKEN_TILES):
-                    last = c == CHUNKS - 1 and j == CHUNK // BANK - 1 and m == TOKEN_TILES - 1
-                    widths = TAIL if last else (BANK,)
-                    col = BANK * j
-                    for width in widths:
-                        acc = psum.tile([P, BANK], F32, name="acc", tag="acc")
-                        for g in range(PASSES):
-                            mx_pass(acc, width, m, g, c, col)
-                        rotate_and_store(acc, width, m, c, col)
-                        col += width
-            if c + 1 + AHEAD < CHUNKS:
-                load_chunk(c + 1 + AHEAD)
+        for n in range(2, UNITS):
+            for m in range(TOKEN_TILES):
+                last = n == UNITS - 1 and m == TOKEN_TILES - 1
+                widths = TAIL if last else (BANK,)
+                col = 0
+                for width in widths:
+                    acc = psum.tile([P, BANK], F32, name="acc", tag="acc")
+                    for g in range(PASSES):
+                        mx_pass(acc, width, m, g, n, col)
+                    rotate_and_store(acc, width, m, n, col)
+                    col += width
+            if n + 2 + LEAD < UNITS:
+                load_unit(n + 2 + LEAD)

@@ -30,7 +30,6 @@ def tile_attention_pa_kernel(tc, x_words, x_scales, wq_words, wq_scales, wk_word
     nc = tc.nc
     with ExitStack() as ctx:
         keep = ctx.enter_context(tc.tile_pool(name="keep", bufs=1))
-        raw_pool = ctx.enter_context(tc.tile_pool(name="raw", bufs=3))
         swap_pool = ctx.enter_context(tc.tile_pool(name="swap", bufs=3))
         res_pool = ctx.enter_context(tc.tile_pool(name="res", bufs=5))
         psum = ctx.enter_context(tc.psum_pool(name="psum", bufs=8))
@@ -147,12 +146,7 @@ def tile_attention_pa_kernel(tc, x_words, x_scales, wq_words, wq_scales, wk_word
         def rotate_and_store(acc, width, m, n, col):
             unused_words, unused_scales, out, c0 = unit_source(n)
             half = width // 2
-            if width == BANK:
-                raw = raw_pool.tile([P, width], F32, name="raw", tag="raw")
-                nc.scalar.copy(out=raw[:], in_=acc[:, 0:width])
-                pairs = raw[:].rearrange("p (i t) -> p i t", t=2)
-            else:
-                pairs = acc[:, 0:width].rearrange("p (i t) -> p i t", t=2)
+            pairs = acc[:, 0:width].rearrange("p (i t) -> p i t", t=2)
             swapped = swap_pool.tile([P, 2, half], F32, name="swapped", tag="swapped")
             nc.scalar.activation(out=swapped[:, 0, :], in_=pairs[:, :, 1], func=ACT.Copy, scale=minus_sin[:, 0:1])
             nc.scalar.activation(out=swapped[:, 1, :], in_=pairs[:, :, 0], func=ACT.Copy, scale=sin)

import math
from contextlib import ExitStack

import concourse.mybir as mybir

F32 = mybir.dt.float32
BF16 = mybir.dt.bfloat16
I32 = mybir.dt.int32
U8 = mybir.dt.uint8
FP4X4 = mybir.dt.float4_e2m1fn_x4
ALU = mybir.AluOpType
ACT = mybir.ActivationFunctionType

P = 128
PASSES = 8
TOKEN_TILES = 4
BANK = 512
UNITS = 16
LEAD = 4
WARM = 9
TAIL = (256, 128, 128,)

FLOPS = 2 * 512 * 4096 * 8192

TWO_PI_HIGH = 6.28125
TWO_PI_LOW = 2.0 * math.pi - TWO_PI_HIGH


def tile_attention_pa_kernel(tc, x_words, x_scales, wq_words, wq_scales, wk_words, wk_scales, out_0, out_1):
    nc = tc.nc
    with ExitStack() as ctx:
        keep = ctx.enter_context(tc.tile_pool(name="keep", bufs=1))
        swap_pool = ctx.enter_context(tc.tile_pool(name="swap", bufs=3))
        res_pool = ctx.enter_context(tc.tile_pool(name="res", bufs=5))
        psum = ctx.enter_context(tc.psum_pool(name="psum", bufs=8))
        ctx.enter_context(tc.manual_schedule())

        def alloc_runs(label, runs, width):
            where = {}
            for g0, g1 in runs:
                t = keep.tile([P, g1 - g0, width], U8, name="%s_%d" % (label, g0), align_bytes=64)
                for g in range(g0, g1):
                    where[g] = (t, g - g0)
            return where

        def load_codes(words, where, g0, g1, b0, width):
            nc.sync.dma_start(
                out=where[g0][0][:].bitcast(I32),
                in_=words[g0:g1, :, b0 : b0 + width].rearrange("g p b -> p g b").bitcast(I32),
            )

        def load_planes(scales, where, g0, g1, c0, width):
            t = where[g0][0]
            nc.vector.memset(t[:].rearrange("p g c -> p (g c)").bitcast(I32), 0)
            for q in range(4):
                nc.sync.dma_start(
                    out=t[32 * q : 32 * q + 4, :, :].bitcast(I32),
                    in_=scales[g0:g1, 4 * q : 4 * q + 4, c0 : c0 + width].rearrange("g r c -> r g c").bitcast(I32),
                )

        def unit_source(n):
            if n < UNITS // 2:
                return wq_words, wq_scales, out_0, BANK * n
            return wk_words, wk_scales, out_1, BANK * (n - UNITS // 2)

        pos = keep.tile([P, 1], F32, name="pos")
        nc.gpsimd.iota(pos[:], pattern=[[0, 1]], base=0, channel_multiplier=1, allow_small_or_imprecise_dtypes=True)
        odd = keep.tile([P, 20], F32, name="odd")
        nc.gpsimd.iota(odd[:], pattern=[[2, 20]], base=1, channel_multiplier=0, allow_small_or_imprecise_dtypes=True)

        x_codes = alloc_runs("xc", ((0, 1), (1, 4), (4, 8)), 2 * 512)
        x_planes = alloc_runs("xp", ((0, 8),), 512)
        pair_codes = alloc_runs("wc01", ((0, 1), (1, 2), (2, 4), (4, 6), (6, 8)), 4 * BANK)
        pair_planes = alloc_runs("wp01", ((0, 2), (2, 8)), 2 * BANK)
        w_codes = {}
        w_planes = {}
        for n in range(2, UNITS):
            w_codes[n] = alloc_runs("wc%d" % n, ((0, 8),), 2 * BANK)
            w_planes[n] = alloc_runs("wp%d" % n, ((0, 8),), BANK)

        def load_unit(n):
            words, scales, unused_out, c0 = unit_source(n)
            load_planes(scales, w_planes[n], 0, 8, c0, BANK)
            load_codes(words, w_codes[n], 0, 8, 2 * c0, 2 * BANK)

        zeros = keep.tile([P, BANK], BF16, name="zeros")
        nc.vector.memset(zeros[:], 0.0)
        load_codes(wq_words, pair_codes, 0, 1, 0, 4 * BANK)
        load_codes(x_words, x_codes, 0, 1, 0, 2 * 512)
        load_planes(wq_scales, pair_planes, 0, 2, 0, 2 * BANK)
        load_planes(x_scales, x_planes, 0, 8, 0, 512)

        idle = psum.tile([P, BANK], F32, name="acc", tag="acc")
        for i in range(WARM):
            nc.tensor.matmul(out=idle[:], lhsT=zeros[:, 0:P], rhs=zeros[:], start=True, stop=True)

        load_codes(wq_words, pair_codes, 1, 2, 0, 4 * BANK)
        load_codes(x_words, x_codes, 1, 4, 0, 2 * 512)
        load_planes(wq_scales, pair_planes, 2, 8, 0, 2 * BANK)
        load_codes(wq_words, pair_codes, 2, 4, 0, 4 * BANK)
        load_codes(wq_words, pair_codes, 4, 6, 0, 4 * BANK)
        load_codes(x_words, x_codes, 4, 8, 0, 2 * 512)
        load_codes(wq_words, pair_codes, 6, 8, 0, 4 * BANK)

        passed = keep.tile([P, 20], F32, name="passed")
        nc.vector.tensor_scalar(out=passed[:], in0=odd[:], scalar1=math.pi, scalar2=pos[:, 0:1], op0=ALU.mult, op1=ALU.is_le)
        turns = keep.tile([P, 1], F32, name="turns")
        nc.vector.tensor_reduce(out=turns[:], in_=passed[:], axis=mybir.AxisListType.X, op=ALU.add)
        coarse = keep.tile([P, 1], F32, name="coarse")
        nc.vector.scalar_tensor_tensor(out=coarse[:], in0=turns[:], scalar=-TWO_PI_HIGH, in1=pos[:], op0=ALU.mult, op1=ALU.add)
        angles = keep.tile([P, 2], F32, name="angles")
        nc.vector.scalar_tensor_tensor(out=angles[:, 0:1], in0=turns[:], scalar=-TWO_PI_LOW, in1=coarse[:], op0=ALU.mult, op1=ALU.add)
        size = keep.tile([P, 1], F32, name="size")
        nc.vector.scalar_tensor_tensor(out=size[:], in0=angles[:, 0:1], scalar=-1.0, in1=angles[:, 0:1], op0=ALU.mult, op1=ALU.max)
        nc.vector.tensor_scalar(out=angles[:, 1:2], in0=size[:], scalar1=-1.0, scalar2=math.pi / 2.0, op0=ALU.mult, op1=ALU.add)
        trig = keep.tile([P, 2], F32, name="trig")
        nc.scalar.activation(out=trig[:], in_=angles[:], func=ACT.Sin)
        minus_sin = keep.tile([P, 1], F32, name="minus_sin")
        nc.vector.tensor_scalar(out=minus_sin[:], in0=trig[:, 0:1], scalar1=-1.0, scalar2=None, op0=ALU.mult)
        sin = trig[:, 0:1]
        cos = trig[:, 1:2]

        for n in range(2, 2 + LEAD):
            load_unit(n)

        def mx_pass(acc, width, m, g, n, col):
            xc, xi = x_codes[g]
            xp, xj = x_planes[g]
            if n < 2:
                wc, wi = pair_codes[g]
                wp, wj = pair_planes[g]
                col = col + BANK * n
            else:
                wc, wi = w_codes[n][g]
                wp, wj = w_planes[n][g]
            nc.tensor.matmul_mx(
                out=acc[:, 0:width],
                lhsT=xc[:, xi, 2 * P * m : 2 * P * (m + 1)].bitcast(FP4X4),
                lhsT_scale=xp[:, xj, P * m : P * (m + 1)],
                rhs=wc[:, wi, 2 * col : 2 * (col + width)].bitcast(FP4X4),
                rhs_scale=wp[:, wj, col : col + width],
                start=(g == 0),
                stop=(g == PASSES - 1),
            )

        def rotate_and_store(acc, width, m, n, col):
            unused_words, unused_scales, out, c0 = unit_source(n)
            half = width // 2
            pairs = acc[:, 0:width].rearrange("p (i t) -> p i t", t=2)
            swapped = swap_pool.tile([P, 2, half], F32, name="swapped", tag="swapped")
            nc.scalar.activation(out=swapped[:, 0, :], in_=pairs[:, :, 1], func=ACT.Copy, scale=minus_sin[:, 0:1])
            nc.scalar.activation(out=swapped[:, 1, :], in_=pairs[:, :, 0], func=ACT.Copy, scale=sin)
            res = res_pool.tile([P, width], F32, name="res", tag="res")
            nc.vector.scalar_tensor_tensor(
                out=res[:].rearrange("p (i t) -> p i t", t=2),
                in0=pairs,
                scalar=cos,
                in1=swapped[:].rearrange("p t i -> p i t"),
                op0=ALU.mult,
                op1=ALU.add,
            )
            nc.sync.dma_start(
                out=out[m].rearrange("t h d -> t (h d)")[:, c0 + col : c0 + col + width],
                in_=res[:],
            )

        first = []
        for n in range(2):
            for m in range(TOKEN_TILES):
                acc = psum.tile([P, BANK], F32, name="acc", tag="acc")
                first.append((acc, m, n))
        for g in range(PASSES):
            for acc, m, n in first:
                mx_pass(acc, BANK, m, g, n, 0)
        for acc, m, n in first:
            rotate_and_store(acc, BANK, m, n, 0)
        for n in range(2 + LEAD, min(4 + LEAD, UNITS)):
            load_unit(n)

        for n in range(2, UNITS):
            for m in range(TOKEN_TILES):
                last = n == UNITS - 1 and m == TOKEN_TILES - 1
                widths = TAIL if last else (BANK,)
                col = 0
                for width in widths:
                    acc = psum.tile([P, BANK], F32, name="acc", tag="acc")
                    for g in range(PASSES):
                        mx_pass(acc, width, m, g, n, col)
                    rotate_and_store(acc, width, m, n, col)
                    col += width
            if n + 2 + LEAD < UNITS:
                load_unit(n + 2 + LEAD)
